import numpy as np
import ml_dtypes


def mxq(x, axis, fmt="e4m3"):
    dtype, down = {"e4m3": (ml_dtypes.float8_e4m3fn, 7), "e5m2": (ml_dtypes.float8_e5m2, 14)}[fmt]
    v = np.moveaxis(np.asarray(x, np.float32).astype(ml_dtypes.bfloat16).astype(np.float64), axis, -1)
    blocks = v.reshape(v.shape[:-1] + (-1, 32))
    amax = np.abs(blocks).max(-1, keepdims=True)
    byte = np.maximum(np.where(amax > 0, np.frexp(amax)[1] - 1 + 127, 0) - down, 1)
    scale = np.exp2(byte - 127.0)
    codes = (blocks / scale).astype(np.float32).astype(dtype).astype(np.float64)
    return np.moveaxis((codes * scale).reshape(v.shape), -1, axis)


WIDE = False


def mx_kscale(k):
    if not WIDE:
        return np.ones(k)
    levels = np.array([30, -30])
    if k % 512:
        return np.exp2(np.random.permutation(np.resize(levels, k // 32))).repeat(32)
    a = np.empty((k // 512, 16))
    for p in range(k // 512):
        a[p, :8] = np.random.permutation(np.resize(levels, 8))
        for g in range(8):
            far = levels[np.abs(levels - a[p, g]) >= 10]
            a[p, g + 8] = far[np.random.randint(len(far))]
    return np.exp2(a.ravel()).repeat(32)


BF16 = ml_dtypes.bfloat16


def bf(x):
    return np.asarray(x, np.float32).astype(BF16)


def f64(x):
    return np.asarray(x).astype(np.float64)


B, S, DIM, H, KV, HD = 1, 512, 2048, 16, 4, 128
ROPE_THETA = 10000.0


def rope_tables():
    inv_freq = 1.0 / ROPE_THETA ** (np.arange(0, HD, 2) / HD)
    freqs = np.outer(np.arange(S), inv_freq)
    return np.cos(freqs), np.sin(freqs)


def rot(t, cos, sin):
    te, to = t[..., 0::2], t[..., 1::2]
    re = te * cos - to * sin
    ro = te * sin + to * cos
    return np.stack((re, ro), axis=-1).reshape(t.shape)


def setup_inputs():
    s = mx_kscale(DIM)
    c, sn = rope_tables()
    return {"x": bf(np.random.standard_normal((B, S, DIM)) * s),
            "wq": bf(np.random.standard_normal((DIM, H * HD)) / np.sqrt(DIM) / s[:, None]),
            "wk": bf(np.random.standard_normal((DIM, KV * HD)) / np.sqrt(DIM) / s[:, None]),
            "wv": bf(np.random.standard_normal((DIM, KV * HD)) / np.sqrt(DIM) / s[:, None]),
            "freqs_cos": bf(c), "freqs_sin": bf(sn)}


def reference(x, wq, wk, wv, freqs_cos, freqs_sin):
    xq = mxq(f64(x), 2, "e5m2")
    q = (xq @ mxq(f64(wq), 0, "e5m2")).reshape(B, S, H, HD)
    k = (xq @ mxq(f64(wk), 0, "e5m2")).reshape(B, S, KV, HD)
    v = (xq @ mxq(f64(wv), 0, "e5m2")).reshape(B, S, KV, HD)
    cos = f64(freqs_cos)[:S][None, :, None, :]
    sin = f64(freqs_sin)[:S][None, :, None, :]
    return rot(q, cos, sin), rot(k, cos, sin), v

@@ -1,0 +1,241 @@
+from contextlib import ExitStack
+
+import concourse.mybir as mybir
+from concourse.masks import make_identity
+
+S, DIM, H, KV, HD = 512, 2048, 16, 4, 128
+FLOPS = 2 * S * DIM * (H + 2 * KV) * HD
+
+F32 = mybir.dt.float32
+BF16 = mybir.dt.bfloat16
+U32 = mybir.dt.uint32
+U8 = mybir.dt.uint8
+FP8X4 = mybir.dt.float8_e5m2_x4
+MULT = mybir.AluOpType.mult
+ADD = mybir.AluOpType.add
+
+P = 128
+PACK = 4
+K_PASS = P * PACK
+PASSES = DIM // K_PASS
+TILES = S // P
+N = 512
+HEADS = N // HD
+RUN = 4
+HEAD_UNITS = 6
+HEAD_SCALAR_COLS = 192
+PAIR_VECTOR_COLS = 128
+
+
+def tile_attention_pa_kernel(tc, x, wq, wk, wv, freqs_cos, freqs_sin, out_0, out_1, out_2):
+    nc = tc.nc
+
+    x_rows = x[0].rearrange("(p j) k -> p j k", j=TILES)
+    q_rows = out_0[0].rearrange("(p j) h d -> p j (h d)", j=TILES)
+    k_rows = out_1[0].rearrange("(p j) h d -> p j (h d)", j=TILES)
+    v_rows = out_2[0].rearrange("(p j) h d -> p j (h d)", j=TILES)
+    groups = [(wk, k_rows)]
+    groups += [(wq[:, n0 : n0 + N], q_rows[:, :, n0 : n0 + N]) for n0 in range(0, H * HD, N)]
+    groups += [(wv, v_rows)]
+    units = len(groups) * PASSES
+    steps = (len(groups) - 1) * TILES
+
+    with ExitStack() as ctx:
+        keep = ctx.enter_context(tc.tile_pool(name="keep", bufs=1))
+        stream = ctx.enter_context(tc.tile_pool(name="stream", bufs=1))
+        psum = ctx.enter_context(tc.psum_pool(name="psum", bufs=1))
+        ctx.enter_context(tc.manual_schedule())
+
+        ident = keep.tile([P, P], F32)
+        make_identity(nc, ident[:])
+        signs = keep.tile([P, 2], F32)
+        nc.vector.memset(signs[:, 0:1], -1.0)
+        nc.vector.memset(signs[:, 1:2], 1.0)
+
+        cos_raw = keep.tile([P, TILES * HD // 2], BF16)
+        sin_raw = keep.tile([P, TILES * HD // 2], BF16)
+        nc.scalar.dma_start(out=cos_raw[:], in_=freqs_cos.rearrange("(p j) i -> p (j i)", j=TILES))
+        nc.scalar.dma_start(out=sin_raw[:], in_=freqs_sin.rearrange("(p j) i -> p (j i)", j=TILES))
+
+        w_raw, w_packed, w_codes, w_scales, x_raw, x_packed, acc, result, cross = {}, {}, {}, {}, {}, {}, {}, {}, {}
+        x_codes = keep.tile([P, TILES, PASSES * P], U32, align_bytes=64)
+        x_scales = keep.tile([P, TILES, PASSES * P], U8, align_bytes=64)
+
+        def load_w(u):
+            g, c = divmod(u, PASSES)
+            w_raw[u] = stream.tile([P, PACK, N], BF16, name="w_raw", bufs=20, align_bytes=64)
+            rows = groups[g][0][c * K_PASS : (c + 1) * K_PASS, :]
+            nc.sync.dma_start(out=w_raw[u][:], in_=rows.rearrange("(p t) n -> p t n", t=PACK))
+
+        def load_x(j):
+            x_raw[j] = stream.tile([P, DIM], BF16, name="x_raw", bufs=TILES, align_bytes=64)
+            nc.sync.dma_start(out=x_raw[j][:], in_=x_rows[:, j, :])
+
+        def packed(u):
+            if u not in w_packed:
+                w_packed[u] = stream.tile([P, N, PACK], BF16, name="w_packed", bufs=5, align_bytes=64)
+            return w_packed[u]
+
+        def pack_runs(copy, u, c0, c1):
+            copy(
+                out=packed(u)[:, c0:c1, :].rearrange("p (c i) t -> p c t i", i=RUN),
+                in_=w_raw[u][:, :, c0:c1].rearrange("p t (c i) -> p c t i", i=RUN),
+            )
+
+        def pack_plain(u, c0, c1):
+            nc.vector.tensor_copy(out=packed(u)[:, c0:c1, :], in_=w_raw[u][:, :, c0:c1].rearrange("p t c -> p c t"))
+
+        def scalar_cols(u):
+            if u < HEAD_UNITS:
+                return HEAD_SCALAR_COLS
+            return N - PAIR_VECTOR_COLS if u % 2 == 1 else N
+
+        def quantize_w(u):
+            w_codes[u] = stream.tile([P, N], U32, name="w_codes", bufs=6, align_bytes=64)
+            w_scales[u] = stream.tile([P, N], U8, name="w_scales", bufs=6, align_bytes=64)
+            nc.vector.quantize_mx(
+                out=w_codes[u][:].bitcast(FP8X4),
+                scales=w_scales[u][:],
+                in_=w_packed[u][:].rearrange("p n t -> p (n t)"),
+            )
+
+        def bank(index):
+            return psum.tile([P, N], F32, name="bank%d" % index)
+
+        def transpose_x(j):
+            words = x_raw[j][:].bitcast(F32)
+            halves = []
+            for half in range(2):
+                turned = bank(TILES + 2 * (j % 2) + half)
+                for slot in range(4):
+                    c, odd = 2 * half + slot // 2, slot % 2
+                    w0 = c * K_PASS // 2
+                    nc.tensor.transpose(
+                        turned[:, slot * P : (slot + 1) * P], words[:, w0 + odd : w0 + K_PASS // 2 : 2], ident[:]
+                    )
+                halves.append(turned)
+            return halves
+
+        def pack_x(j, halves):
+            x_packed[j] = stream.tile([P, DIM], BF16, name="x_packed", bufs=2, align_bytes=64)
+            words = x_packed[j][:].bitcast(F32)
+            for half, turned in enumerate(halves):
+                nc.scalar.copy(
+                    out=words[:, half * N : (half + 1) * N].rearrange("p (c r u) -> p c r u", c=2, u=2),
+                    in_=turned[:].rearrange("p (c u r) -> p c r u", c=2, u=2),
+                )
+
+        def quantize_x(j):
+            nc.vector.quantize_mx(out=x_codes[:, j, :].bitcast(FP8X4), scales=x_scales[:, j, :], in_=x_packed[j][:])
+
+        def multiply(u, j):
+            g, c = divmod(u, PASSES)
+            if c == 0:
+                acc[g, j] = bank(TILES * (g % 2) + j)
+            cols = slice(c * P, (c + 1) * P)
+            nc.tensor.matmul_mx(
+                out=acc[g, j][:],
+                lhsT=x_codes[:, j, cols].bitcast(FP8X4),
+                lhsT_scale=x_scales[:, j, cols],
+                rhs=w_codes[u][:].bitcast(FP8X4),
+                rhs_scale=w_scales[u][:],
+                start=(c == 0),
+                stop=(c == PASSES - 1),
+            )
+
+        def out_tile(g):
+            if g not in result:
+                result[g] = keep.tile([P, TILES, N], F32, name="result%d" % g)
+            return result[g]
+
+        def times_cos(g, j):
+            nc.vector.tensor_tensor(
+                out=out_tile(g)[:, j, :].rearrange("p (h d) -> p h d", h=HEADS),
+                in0=acc[g, j][:].rearrange("p (h d) -> p h d", h=HEADS),
+                in1=cos_pairs[:, j, :].unsqueeze(1).to_broadcast([P, HEADS, HD]),
+                op=MULT,
+            )
+
+        def times_sin(g, j):
+            cross[g, j] = stream.tile([P, N], F32, name="cross", bufs=3)
+            nc.vector.tensor_tensor(
+                out=cross[g, j][:].rearrange("p (h i e) -> p h i e", h=HEADS, e=2),
+                in0=acc[g, j][:].rearrange("p (h i e) -> p h i e", h=HEADS, e=2)[:, :, :, ::-1],
+                in1=sin_pairs[:, j, :].rearrange("p (i e) -> p i e", e=2).unsqueeze(1).to_broadcast([P, HEADS, HD // 2, 2]),
+                op=MULT,
+            )
+
+        def add_cross(engine, g, j):
+            engine.tensor_tensor(out=result[g][:, j, :], in0=result[g][:, j, :], in1=cross[g, j][:], op=ADD)
+
+        for j in range(TILES):
+            load_w(j)
+            load_x(j)
+        for u in range(PASSES, 20):
+            load_w(u)
+
+        cos_pairs = keep.tile([P, TILES, HD], F32)
+        sin_pairs = keep.tile([P, TILES, HD], F32)
+        pairs = TILES * HD // 2
+        nc.vector.tensor_copy(
+            out=cos_pairs[:].rearrange("p j (i e) -> p (j i) e", e=2),
+            in_=cos_raw[:].unsqueeze(2).to_broadcast([P, pairs, 2]),
+        )
+        nc.vector.tensor_tensor(
+            out=sin_pairs[:].rearrange("p j (i e) -> p (j i) e", e=2),
+            in0=sin_raw[:].unsqueeze(2).to_broadcast([P, pairs, 2]),
+            in1=signs[:].unsqueeze(1).to_broadcast([P, pairs, 2]),
+            op=MULT,
+        )
+
+        turned_x = {0: transpose_x(0)}
+        for u in range(TILES + 1):
+            pack_runs(nc.scalar.copy, u, 0, HEAD_SCALAR_COLS)
+            pack_runs(nc.vector.tensor_copy, u, HEAD_SCALAR_COLS, N)
+            quantize_w(u)
+            if u > 0:
+                j = u - 1
+                pack_x(j, turned_x[j])
+                quantize_x(j)
+                if u < TILES:
+                    turned_x[u] = transpose_x(u)
+                for jj in range(j):
+                    multiply(j, jj)
+                for c in range(j + 1):
+                    multiply(c, j)
+        for j in range(TILES):
+            multiply(TILES, j)
+        for u in range(20, units):
+            load_w(u)
+
+        first = TILES + 1
+        for s in range(steps):
+            g, j = divmod(s, TILES)
+            u = first + s
+            if u < units:
+                pack_runs(nc.scalar.copy, u, 0, scalar_cols(u))
+            if u < HEAD_UNITS:
+                pack_runs(nc.vector.tensor_copy, u, HEAD_SCALAR_COLS, N)
+            times_cos(g, j)
+            cut = N - PAIR_VECTOR_COLS // 2 + 1
+            if u % 2 == 0 and u + 1 < units:
+                pack_plain(u + 1, N - PAIR_VECTOR_COLS, cut)
+            if u % 2 == 1 and HEAD_UNITS <= u < units:
+                pack_plain(u, cut, N)
+            times_sin(g, j)
+            if u < units:
+                quantize_w(u)
+                for jj in range(TILES):
+                    multiply(u, jj)
+            add_cross(nc.gpsimd if s < steps - 1 else nc.vector, g, j)
+            if g < len(groups) - 2:
+                if j == TILES - 1:
+                    nc.sync.dma_start(out=groups[g][1], in_=result[g][:])
+            else:
+                nc.sync.dma_start(out=groups[g][1][:, j, :], in_=result[g][:, j, :])
+
+        g = len(groups) - 1
+        for j in range(TILES):
+            copy = nc.scalar.copy if j < TILES - 1 else nc.vector.tensor_copy
+            copy(out=out_tile(g)[:, j, :], in_=acc[g, j][:])
+            nc.sync.dma_start(out=groups[g][1][:, j, :], in_=result[g][:, j, :])

@@ -22,9 +22,10 @@ TILES = S // P
 N = 512
 HEADS = N // HD
 RUN = 4
-HEAD_UNITS = 6
+RAW_BUFS = 16
 HEAD_SCALAR_COLS = 192
-PAIR_VECTOR_COLS = 128
+EXTRA_VECTOR_COLS = 256
+SHARED_VECTOR_COLS = 160
 
 
 def tile_attention_pa_kernel(tc, x, wq, wk, wv, freqs_cos, freqs_sin, out_0, out_1, out_2):
@@ -37,8 +38,8 @@ def tile_attention_pa_kernel(tc, x, wq, wk, wv, freqs_cos, freqs_sin, out_0, out
     groups = [(wk, k_rows)]
     groups += [(wq[:, n0 : n0 + N], q_rows[:, :, n0 : n0 + N]) for n0 in range(0, H * HD, N)]
     groups += [(wv, v_rows)]
-    units = len(groups) * PASSES
-    steps = (len(groups) - 1) * TILES
+    slabs = len(groups) * PASSES
+    turns = (len(groups) - 1) * TILES
 
     with ExitStack() as ctx:
         keep = ctx.enter_context(tc.tile_pool(name="keep", bufs=1))
@@ -49,21 +50,22 @@ def tile_attention_pa_kernel(tc, x, wq, wk, wv, freqs_cos, freqs_sin, out_0, out
         ident = keep.tile([P, P], F32)
         make_identity(nc, ident[:])
         signs = keep.tile([P, 2], F32)
-        nc.vector.memset(signs[:, 0:1], -1.0)
-        nc.vector.memset(signs[:, 1:2], 1.0)
+        nc.vector.memset(signs[:, 0:1], 1.0)
+        nc.vector.memset(signs[:, 1:2], -1.0)
 
         cos_raw = keep.tile([P, TILES * HD // 2], BF16)
         sin_raw = keep.tile([P, TILES * HD // 2], BF16)
         nc.scalar.dma_start(out=cos_raw[:], in_=freqs_cos.rearrange("(p j) i -> p (j i)", j=TILES))
         nc.scalar.dma_start(out=sin_raw[:], in_=freqs_sin.rearrange("(p j) i -> p (j i)", j=TILES))
 
-        w_raw, w_packed, w_codes, w_scales, x_raw, x_packed, acc, result, cross = {}, {}, {}, {}, {}, {}, {}, {}, {}
+        w_raw, w_packed, w_codes, w_scales = {}, {}, {}, {}
+        x_raw, x_turned, x_packed, acc, result, products = {}, {}, {}, {}, {}, {}
         x_codes = keep.tile([P, TILES, PASSES * P], U32, align_bytes=64)
         x_scales = keep.tile([P, TILES, PASSES * P], U8, align_bytes=64)
 
         def load_w(u):
             g, c = divmod(u, PASSES)
-            w_raw[u] = stream.tile([P, PACK, N], BF16, name="w_raw", bufs=20, align_bytes=64)
+            w_raw[u] = stream.tile([P, PACK, N], BF16, name="w_raw", bufs=RAW_BUFS, align_bytes=64)
             rows = groups[g][0][c * K_PASS : (c + 1) * K_PASS, :]
             nc.sync.dma_start(out=w_raw[u][:], in_=rows.rearrange("(p t) n -> p t n", t=PACK))
 
@@ -72,31 +74,31 @@ def tile_attention_pa_kernel(tc, x, wq, wk, wv, freqs_cos, freqs_sin, out_0, out
             nc.sync.dma_start(out=x_raw[j][:], in_=x_rows[:, j, :])
 
         def packed(u):
-            if u not in w_packed:
-                w_packed[u] = stream.tile([P, N, PACK], BF16, name="w_packed", bufs=5, align_bytes=64)
-            return w_packed[u]
+            if u // 2 not in w_packed:
+                w_packed[u // 2] = stream.tile([P, 2, N, PACK], BF16, name="w_packed", bufs=5, align_bytes=64)
+            return w_packed[u // 2][:, u % 2]
 
-        def pack_runs(copy, u, c0, c1):
+        def pack_w(copy, u, c0=0, c1=N):
             copy(
                 out=packed(u)[:, c0:c1, :].rearrange("p (c i) t -> p c t i", i=RUN),
                 in_=w_raw[u][:, :, c0:c1].rearrange("p t (c i) -> p c t i", i=RUN),
             )
 
-        def pack_plain(u, c0, c1):
-            nc.vector.tensor_copy(out=packed(u)[:, c0:c1, :], in_=w_raw[u][:, :, c0:c1].rearrange("p t c -> p c t"))
+        def pack_w_one_port(u, c0, c1):
+            nc.vector.tensor_copy(
+                out=packed(u)[:, c0:c1, :], in_=w_raw[u][:, :, c0:c1].rearrange("p t c -> p c t")
+            )
 
-        def scalar_cols(u):
-            if u < HEAD_UNITS:
-                return HEAD_SCALAR_COLS
-            return N - PAIR_VECTOR_COLS if u % 2 == 1 else N
-
-        def quantize_w(u):
-            w_codes[u] = stream.tile([P, N], U32, name="w_codes", bufs=6, align_bytes=64)
-            w_scales[u] = stream.tile([P, N], U8, name="w_scales", bufs=6, align_bytes=64)
+        def quantize_w(u, count):
+            pair, lo = divmod(u, 2)
+            if pair not in w_codes:
+                w_codes[pair] = stream.tile([P, 2 * N], U32, name="w_codes", bufs=4, align_bytes=64)
+                w_scales[pair] = stream.tile([P, 2 * N], U8, name="w_scales", bufs=4, align_bytes=64)
+            cols = slice(lo * N, (lo + count) * N)
             nc.vector.quantize_mx(
-                out=w_codes[u][:].bitcast(FP8X4),
-                scales=w_scales[u][:],
-                in_=w_packed[u][:].rearrange("p n t -> p (n t)"),
+                out=w_codes[pair][:, cols].bitcast(FP8X4),
+                scales=w_scales[pair][:, cols],
+                in_=w_packed[pair][:, lo : lo + count].rearrange("p s n t -> p (s n t)"),
             )
 
         def bank(index):
@@ -104,7 +106,7 @@ def tile_attention_pa_kernel(tc, x, wq, wk, wv, freqs_cos, freqs_sin, out_0, out
 
         def transpose_x(j):
             words = x_raw[j][:].bitcast(F32)
-            halves = []
+            x_turned[j] = []
             for half in range(2):
                 turned = bank(TILES + 2 * (j % 2) + half)
                 for slot in range(4):
@@ -113,13 +115,12 @@ def tile_attention_pa_kernel(tc, x, wq, wk, wv, freqs_cos, freqs_sin, out_0, out
                     nc.tensor.transpose(
                         turned[:, slot * P : (slot + 1) * P], words[:, w0 + odd : w0 + K_PASS // 2 : 2], ident[:]
                     )
-                halves.append(turned)
-            return halves
+                x_turned[j].append(turned)
 
-        def pack_x(j, halves):
+        def pack_x(j):
             x_packed[j] = stream.tile([P, DIM], BF16, name="x_packed", bufs=2, align_bytes=64)
             words = x_packed[j][:].bitcast(F32)
-            for half, turned in enumerate(halves):
+            for half, turned in enumerate(x_turned[j]):
                 nc.scalar.copy(
                     out=words[:, half * N : (half + 1) * N].rearrange("p (c r u) -> p c r u", c=2, u=2),
                     in_=turned[:].rearrange("p (c u r) -> p c r u", c=2, u=2),
@@ -132,110 +133,137 @@ def tile_attention_pa_kernel(tc, x, wq, wk, wv, freqs_cos, freqs_sin, out_0, out
             g, c = divmod(u, PASSES)
             if c == 0:
                 acc[g, j] = bank(TILES * (g % 2) + j)
-            cols = slice(c * P, (c + 1) * P)
+            x_cols = slice(c * P, (c + 1) * P)
+            w_cols = slice(u % 2 * N, (u % 2 + 1) * N)
             nc.tensor.matmul_mx(
                 out=acc[g, j][:],
-                lhsT=x_codes[:, j, cols].bitcast(FP8X4),
-                lhsT_scale=x_scales[:, j, cols],
-                rhs=w_codes[u][:].bitcast(FP8X4),
-                rhs_scale=w_scales[u][:],
+                lhsT=x_codes[:, j, x_cols].bitcast(FP8X4),
+                lhsT_scale=x_scales[:, j, x_cols],
+                rhs=w_codes[u // 2][:, w_cols].bitcast(FP8X4),
+                rhs_scale=w_scales[u // 2][:, w_cols],
                 start=(c == 0),
                 stop=(c == PASSES - 1),
             )
 
+        def quantize_and_multiply(u):
+            quantize_w(u, 2)
+            if u + 2 < slabs:
+                order = [(uu, j) for uu in (u, u + 1) for j in range(TILES)]
+            else:
+                order = [(uu, j) for j in range(TILES) for uu in (u, u + 1)]
+            for uu, j in order:
+                multiply(uu, j)
+
         def out_tile(g):
             if g not in result:
-                result[g] = keep.tile([P, TILES, N], F32, name="result%d" % g)
+                result[g] = stream.tile([P, TILES, N], F32, name="result", bufs=5)
             return result[g]
 
-        def times_cos(g, j):
+        def scale(s):
+            g, j = divmod(s, TILES)
+            if s % 2 == 0:
+                products[s // 2] = stream.tile([P, 2, 2, N], F32, name="products", bufs=3)
             nc.vector.tensor_tensor(
-                out=out_tile(g)[:, j, :].rearrange("p (h d) -> p h d", h=HEADS),
-                in0=acc[g, j][:].rearrange("p (h d) -> p h d", h=HEADS),
-                in1=cos_pairs[:, j, :].unsqueeze(1).to_broadcast([P, HEADS, HD]),
+                out=products[s // 2][:, :, s % 2, :].rearrange("p w (h d) -> p w h d", h=HEADS),
+                in0=acc[g, j][:].rearrange("p (h d) -> p h d", h=HEADS).unsqueeze(1).to_broadcast([P, 2, HEADS, HD]),
+                in1=table[:, :, j, :].unsqueeze(2).to_broadcast([P, 2, HEADS, HD]),
                 op=MULT,
             )
 
-        def times_sin(g, j):
-            cross[g, j] = stream.tile([P, N], F32, name="cross", bufs=3)
-            nc.vector.tensor_tensor(
-                out=cross[g, j][:].rearrange("p (h i e) -> p h i e", h=HEADS, e=2),
-                in0=acc[g, j][:].rearrange("p (h i e) -> p h i e", h=HEADS, e=2)[:, :, :, ::-1],
-                in1=sin_pairs[:, j, :].rearrange("p (i e) -> p i e", e=2).unsqueeze(1).to_broadcast([P, HEADS, HD // 2, 2]),
-                op=MULT,
+        def combine(engine, s, count):
+            g, j = divmod(s, TILES)
+            both = products[s // 2][:, :, s % 2 : s % 2 + count, :]
+            engine.tensor_tensor(
+                out=out_tile(g)[:, j : j + count, :].rearrange("p b (m e) -> p (b m) e", e=2),
+                in0=both[:, 0].rearrange("p b (m e) -> p (b m) e", e=2),
+                in1=both[:, 1].rearrange("p b (m e) -> p (b m) e", e=2)[:, :, ::-1],
+                op=ADD,
             )
 
-        def add_cross(engine, g, j):
-            engine.tensor_tensor(out=result[g][:, j, :], in0=result[g][:, j, :], in1=cross[g, j][:], op=ADD)
+        def store(queue, g, j0, j1):
+            queue.dma_start(out=groups[g][1][:, j0:j1, :], in_=result[g][:, j0:j1, :])
 
         for j in range(TILES):
             load_w(j)
             load_x(j)
-        for u in range(PASSES, 20):
+        for u in range(PASSES, RAW_BUFS):
             load_w(u)
 
-        cos_pairs = keep.tile([P, TILES, HD], F32)
-        sin_pairs = keep.tile([P, TILES, HD], F32)
+        table = keep.tile([P, 2, TILES, HD], F32)
         pairs = TILES * HD // 2
         nc.vector.tensor_copy(
-            out=cos_pairs[:].rearrange("p j (i e) -> p (j i) e", e=2),
+            out=table[:, 0].rearrange("p j (i e) -> p (j i) e", e=2),
             in_=cos_raw[:].unsqueeze(2).to_broadcast([P, pairs, 2]),
         )
         nc.vector.tensor_tensor(
-            out=sin_pairs[:].rearrange("p j (i e) -> p (j i) e", e=2),
+            out=table[:, 1].rearrange("p j (i e) -> p (j i) e", e=2),
             in0=sin_raw[:].unsqueeze(2).to_broadcast([P, pairs, 2]),
             in1=signs[:].unsqueeze(1).to_broadcast([P, pairs, 2]),
             op=MULT,
         )
 
-        turned_x = {0: transpose_x(0)}
-        for u in range(TILES + 1):
-            pack_runs(nc.scalar.copy, u, 0, HEAD_SCALAR_COLS)
-            pack_runs(nc.vector.tensor_copy, u, HEAD_SCALAR_COLS, N)
-            quantize_w(u)
+        transpose_x(0)
+        for u in range(PASSES):
+            pack_w(nc.scalar.copy, u, 0, HEAD_SCALAR_COLS)
+            pack_w(nc.vector.tensor_copy, u, HEAD_SCALAR_COLS, N)
             if u > 0:
-                j = u - 1
-                pack_x(j, turned_x[j])
-                quantize_x(j)
-                if u < TILES:
-                    turned_x[u] = transpose_x(u)
-                for jj in range(j):
-                    multiply(j, jj)
-                for c in range(j + 1):
-                    multiply(c, j)
-        for j in range(TILES):
-            multiply(TILES, j)
-        for u in range(20, units):
+                pack_x(u - 1)
+            quantize_w(u, 1)
+            if u > 0:
+                quantize_x(u - 1)
+                for c in range(u):
+                    multiply(c, u - 1)
+                for j in range(u):
+                    multiply(u, j)
+            if u + 1 < TILES:
+                transpose_x(u + 1)
+        pack_w(nc.vector.tensor_copy, 4)
+        pack_x(TILES - 1)
+        quantize_x(TILES - 1)
+        for c in range(PASSES):
+            multiply(c, TILES - 1)
+        pack_w(nc.scalar.copy, 5)
+        pack_w(nc.vector.tensor_copy, 6)
+        quantize_and_multiply(4)
+        pack_w(nc.scalar.copy, 7)
+        pack_w(nc.vector.tensor_copy, 8)
+        pack_w(nc.vector.tensor_copy, 9, N - EXTRA_VECTOR_COLS, N)
+        pack_w(nc.scalar.copy, 9, 0, N - EXTRA_VECTOR_COLS)
+        for u in range(RAW_BUFS, slabs):
             load_w(u)
 
-        first = TILES + 1
-        for s in range(steps):
+        last = len(groups) - 1
+        shared_from = N - SHARED_VECTOR_COLS
+        shared_cut = N - SHARED_VECTOR_COLS // 2 + 1
+        for s in range(0, turns, 2):
             g, j = divmod(s, TILES)
-            u = first + s
-            if u < units:
-                pack_runs(nc.scalar.copy, u, 0, scalar_cols(u))
-            if u < HEAD_UNITS:
-                pack_runs(nc.vector.tensor_copy, u, HEAD_SCALAR_COLS, N)
-            times_cos(g, j)
-            cut = N - PAIR_VECTOR_COLS // 2 + 1
-            if u % 2 == 0 and u + 1 < units:
-                pack_plain(u + 1, N - PAIR_VECTOR_COLS, cut)
-            if u % 2 == 1 and HEAD_UNITS <= u < units:
-                pack_plain(u, cut, N)
-            times_sin(g, j)
-            if u < units:
-                quantize_w(u)
-                for jj in range(TILES):
-                    multiply(u, jj)
-            add_cross(nc.gpsimd if s < steps - 1 else nc.vector, g, j)
-            if g < len(groups) - 2:
-                if j == TILES - 1:
-                    nc.sync.dma_start(out=groups[g][1], in_=result[g][:])
+            u = s + 6
+            if 10 <= u < slabs:
+                pack_w(nc.scalar.copy, u)
+                pack_w(nc.scalar.copy, u + 1, 0, shared_from if j == 0 else N)
+            scale(s)
+            if j == 2 and u + 3 < slabs:
+                pack_w_one_port(u + 3, shared_from, shared_cut)
+            if j == 0 and s > 0:
+                pack_w_one_port(u + 1, shared_cut, N)
+            scale(s + 1)
+            if u < slabs:
+                quantize_and_multiply(u)
+            if s < turns - 4:
+                combine(nc.gpsimd, s, 2)
+                if g >= 2:
+                    store(nc.sync, g, j, j + 2)
+                elif j == 2:
+                    store(nc.sync, g, 0, TILES)
+            elif s < turns - 2:
+                for b in range(2):
+                    combine(nc.gpsimd, s + 1 - b, 1)
+                    for jv in (2 * b, 2 * b + 1):
+                        nc.scalar.copy(out=out_tile(last)[:, jv, :], in_=acc[last, jv][:])
+                    store(nc.sync, last, 2 * b, 2 * b + 1)
+                    store(nc.sync, g, j + 1 - b, j + 2 - b)
+                    store(nc.sync, last, 2 * b + 1, 2 * b + 2)
             else:
-                nc.sync.dma_start(out=groups[g][1][:, j, :], in_=result[g][:, j, :])
-
-        g = len(groups) - 1
-        for j in range(TILES):
-            copy = nc.scalar.copy if j < TILES - 1 else nc.vector.tensor_copy
-            copy(out=out_tile(g)[:, j, :], in_=acc[g, j][:])
-            nc.sync.dma_start(out=groups[g][1][:, j, :], in_=result[g][:, j, :])
+                for b in range(2):
+                    combine(nc.vector, s + b, 1)
+                    store(nc.sync, g, j + b, j + b + 1)

@@ -24,8 +24,8 @@ HEADS = N // HD
 RUN = 4
 RAW_BUFS = 16
 HEAD_SCALAR_COLS = 192
-EXTRA_VECTOR_COLS = 256
-SHARED_VECTOR_COLS = 160
+EXTRA_VECTOR_COLS = 0
+SHARED_VECTOR_COLS = 0
 
 
 def tile_attention_pa_kernel(tc, x, wq, wk, wv, freqs_cos, freqs_sin, out_0, out_1, out_2):
@@ -184,8 +184,8 @@ def tile_attention_pa_kernel(tc, x, wq, wk, wv, freqs_cos, freqs_sin, out_0, out
             queue.dma_start(out=groups[g][1][:, j0:j1, :], in_=result[g][:, j0:j1, :])
 
         for j in range(TILES):
-            load_w(j)
             load_x(j)
+            load_w(j)
         for u in range(PASSES, RAW_BUFS):
             load_w(u)
 
@@ -204,31 +204,26 @@ def tile_attention_pa_kernel(tc, x, wq, wk, wv, freqs_cos, freqs_sin, out_0, out
 
         transpose_x(0)
         for u in range(PASSES):
-            pack_w(nc.scalar.copy, u, 0, HEAD_SCALAR_COLS)
-            pack_w(nc.vector.tensor_copy, u, HEAD_SCALAR_COLS, N)
-            if u > 0:
-                pack_x(u - 1)
-            quantize_w(u, 1)
-            if u > 0:
-                quantize_x(u - 1)
-                for c in range(u):
-                    multiply(c, u - 1)
-                for j in range(u):
-                    multiply(u, j)
             if u + 1 < TILES:
                 transpose_x(u + 1)
+            pack_x(u)
+            pack_w(nc.scalar.copy, u, 0, HEAD_SCALAR_COLS)
+            pack_w(nc.vector.tensor_copy, u, HEAD_SCALAR_COLS, N)
+            quantize_x(u)
+            quantize_w(u, 1)
+            for c in range(u):
+                multiply(c, u)
+            for j in range(u + 1):
+                multiply(u, j)
         pack_w(nc.vector.tensor_copy, 4)
-        pack_x(TILES - 1)
-        quantize_x(TILES - 1)
-        for c in range(PASSES):
-            multiply(c, TILES - 1)
         pack_w(nc.scalar.copy, 5)
         pack_w(nc.vector.tensor_copy, 6)
         quantize_and_multiply(4)
         pack_w(nc.scalar.copy, 7)
         pack_w(nc.vector.tensor_copy, 8)
-        pack_w(nc.vector.tensor_copy, 9, N - EXTRA_VECTOR_COLS, N)
-        pack_w(nc.scalar.copy, 9, 0, N - EXTRA_VECTOR_COLS)
+
+        pack_w(nc.scalar.copy, 9)
+        pack_w(nc.vector.tensor_copy, 10, N - 512, N)
         for u in range(RAW_BUFS, slabs):
             load_w(u)
 
@@ -239,13 +234,10 @@ def tile_attention_pa_kernel(tc, x, wq, wk, wv, freqs_cos, freqs_sin, out_0, out
             g, j = divmod(s, TILES)
             u = s + 6
             if 10 <= u < slabs:
-                pack_w(nc.scalar.copy, u)
-                pack_w(nc.scalar.copy, u + 1, 0, shared_from if j == 0 else N)
+                if u > 10:
+                    pack_w(nc.scalar.copy, u)
+                pack_w(nc.scalar.copy, u + 1)
             scale(s)
-            if j == 2 and u + 3 < slabs:
-                pack_w_one_port(u + 3, shared_from, shared_cut)
-            if j == 0 and s > 0:
-                pack_w_one_port(u + 1, shared_cut, N)
             scale(s + 1)
             if u < slabs:
                 quantize_and_multiply(u)

@@ -22,10 +22,16 @@ TILES = S // P
 N = 512
 HEADS = N // HD
 RUN = 4
-RAW_BUFS = 16
-HEAD_SCALAR_COLS = 192
-EXTRA_VECTOR_COLS = 0
-SHARED_VECTOR_COLS = 0
+
+RAW_SLABS = 16
+PACKED_PAIRS = 5
+CODE_PAIRS = 4
+RESULT_TILES = 5
+PRODUCT_PAIRS = 3
+
+FIRST_GROUP_SCALAR_COLS = 192
+LAST_VECTOR_SLAB = 10
+LEAD = 6
 
 
 def tile_attention_pa_kernel(tc, x, wq, wk, wv, freqs_cos, freqs_sin, out_0, out_1, out_2):
@@ -38,8 +44,9 @@ def tile_attention_pa_kernel(tc, x, wq, wk, wv, freqs_cos, freqs_sin, out_0, out
     groups = [(wk, k_rows)]
     groups += [(wq[:, n0 : n0 + N], q_rows[:, :, n0 : n0 + N]) for n0 in range(0, H * HD, N)]
     groups += [(wv, v_rows)]
+    v_group = len(groups) - 1
     slabs = len(groups) * PASSES
-    turns = (len(groups) - 1) * TILES
+    turns = v_group * TILES
 
     with ExitStack() as ctx:
         keep = ctx.enter_context(tc.tile_pool(name="keep", bufs=1))
@@ -65,7 +72,7 @@ def tile_attention_pa_kernel(tc, x, wq, wk, wv, freqs_cos, freqs_sin, out_0, out
 
         def load_w(u):
             g, c = divmod(u, PASSES)
-            w_raw[u] = stream.tile([P, PACK, N], BF16, name="w_raw", bufs=RAW_BUFS, align_bytes=64)
+            w_raw[u] = stream.tile([P, PACK, N], BF16, name="w_raw", bufs=RAW_SLABS, align_bytes=64)
             rows = groups[g][0][c * K_PASS : (c + 1) * K_PASS, :]
             nc.sync.dma_start(out=w_raw[u][:], in_=rows.rearrange("(p t) n -> p t n", t=PACK))
 
@@ -73,32 +80,25 @@ def tile_attention_pa_kernel(tc, x, wq, wk, wv, freqs_cos, freqs_sin, out_0, out
             x_raw[j] = stream.tile([P, DIM], BF16, name="x_raw", bufs=TILES, align_bytes=64)
             nc.sync.dma_start(out=x_raw[j][:], in_=x_rows[:, j, :])
 
-        def packed(u):
-            if u // 2 not in w_packed:
-                w_packed[u // 2] = stream.tile([P, 2, N, PACK], BF16, name="w_packed", bufs=5, align_bytes=64)
-            return w_packed[u // 2][:, u % 2]
-
         def pack_w(copy, u, c0=0, c1=N):
+            pair, half = divmod(u, 2)
+            if pair not in w_packed:
+                w_packed[pair] = stream.tile([P, 2, N, PACK], BF16, name="w_packed", bufs=PACKED_PAIRS, align_bytes=64)
             copy(
-                out=packed(u)[:, c0:c1, :].rearrange("p (c i) t -> p c t i", i=RUN),
+                out=w_packed[pair][:, half][:, c0:c1, :].rearrange("p (c i) t -> p c t i", i=RUN),
                 in_=w_raw[u][:, :, c0:c1].rearrange("p t (c i) -> p c t i", i=RUN),
             )
 
-        def pack_w_one_port(u, c0, c1):
-            nc.vector.tensor_copy(
-                out=packed(u)[:, c0:c1, :], in_=w_raw[u][:, :, c0:c1].rearrange("p t c -> p c t")
-            )
-
         def quantize_w(u, count):
-            pair, lo = divmod(u, 2)
+            pair, half = divmod(u, 2)
             if pair not in w_codes:
-                w_codes[pair] = stream.tile([P, 2 * N], U32, name="w_codes", bufs=4, align_bytes=64)
-                w_scales[pair] = stream.tile([P, 2 * N], U8, name="w_scales", bufs=4, align_bytes=64)
-            cols = slice(lo * N, (lo + count) * N)
+                w_codes[pair] = stream.tile([P, 2 * N], U32, name="w_codes", bufs=CODE_PAIRS, align_bytes=64)
+                w_scales[pair] = stream.tile([P, 2 * N], U8, name="w_scales", bufs=CODE_PAIRS, align_bytes=64)
+            cols = slice(half * N, (half + count) * N)
             nc.vector.quantize_mx(
                 out=w_codes[pair][:, cols].bitcast(FP8X4),
                 scales=w_scales[pair][:, cols],
-                in_=w_packed[pair][:, lo : lo + count].rearrange("p s n t -> p (s n t)"),
+                in_=w_packed[pair][:, half : half + count].rearrange("p s n t -> p (s n t)"),
             )
 
         def bank(index):
@@ -106,14 +106,14 @@ def tile_attention_pa_kernel(tc, x, wq, wk, wv, freqs_cos, freqs_sin, out_0, out
 
         def transpose_x(j):
             words = x_raw[j][:].bitcast(F32)
+            pass_words = K_PASS // 2
             x_turned[j] = []
             for half in range(2):
                 turned = bank(TILES + 2 * (j % 2) + half)
                 for slot in range(4):
-                    c, odd = 2 * half + slot // 2, slot % 2
-                    w0 = c * K_PASS // 2
+                    w0 = (2 * half + slot // 2) * pass_words
                     nc.tensor.transpose(
-                        turned[:, slot * P : (slot + 1) * P], words[:, w0 + odd : w0 + K_PASS // 2 : 2], ident[:]
+                        turned[:, slot * P : (slot + 1) * P], words[:, w0 + slot % 2 : w0 + pass_words : 2], ident[:]
                     )
                 x_turned[j].append(turned)
 
@@ -122,8 +122,8 @@ def tile_attention_pa_kernel(tc, x, wq, wk, wv, freqs_cos, freqs_sin, out_0, out
             words = x_packed[j][:].bitcast(F32)
             for half, turned in enumerate(x_turned[j]):
                 nc.scalar.copy(
-                    out=words[:, half * N : (half + 1) * N].rearrange("p (c r u) -> p c r u", c=2, u=2),
-                    in_=turned[:].rearrange("p (c u r) -> p c r u", c=2, u=2),
+                    out=words[:, half * N : (half + 1) * N].rearrange("p (c r o) -> p c r o", c=2, o=2),
+                    in_=turned[:].rearrange("p (c o r) -> p c r o", c=2, o=2),
                 )
 
         def quantize_x(j):
@@ -148,21 +148,21 @@ def tile_attention_pa_kernel(tc, x, wq, wk, wv, freqs_cos, freqs_sin, out_0, out
         def quantize_and_multiply(u):
             quantize_w(u, 2)
             if u + 2 < slabs:
-                order = [(uu, j) for uu in (u, u + 1) for j in range(TILES)]
+                order = [(slab, j) for slab in (u, u + 1) for j in range(TILES)]
             else:
-                order = [(uu, j) for j in range(TILES) for uu in (u, u + 1)]
-            for uu, j in order:
-                multiply(uu, j)
+                order = [(slab, j) for j in range(TILES) for slab in (u, u + 1)]
+            for slab, j in order:
+                multiply(slab, j)
 
         def out_tile(g):
             if g not in result:
-                result[g] = stream.tile([P, TILES, N], F32, name="result", bufs=5)
+                result[g] = stream.tile([P, TILES, N], F32, name="result", bufs=RESULT_TILES)
             return result[g]
 
-        def scale(s):
+        def rotation_products(s):
             g, j = divmod(s, TILES)
             if s % 2 == 0:
-                products[s // 2] = stream.tile([P, 2, 2, N], F32, name="products", bufs=3)
+                products[s // 2] = stream.tile([P, 2, 2, N], F32, name="products", bufs=PRODUCT_PAIRS)
             nc.vector.tensor_tensor(
                 out=products[s // 2][:, :, s % 2, :].rearrange("p w (h d) -> p w h d", h=HEADS),
                 in0=acc[g, j][:].rearrange("p (h d) -> p h d", h=HEADS).unsqueeze(1).to_broadcast([P, 2, HEADS, HD]),
@@ -170,7 +170,7 @@ def tile_attention_pa_kernel(tc, x, wq, wk, wv, freqs_cos, freqs_sin, out_0, out
                 op=MULT,
             )
 
-        def combine(engine, s, count):
+        def rotation_sum(engine, s, count):
             g, j = divmod(s, TILES)
             both = products[s // 2][:, :, s % 2 : s % 2 + count, :]
             engine.tensor_tensor(
@@ -180,25 +180,25 @@ def tile_attention_pa_kernel(tc, x, wq, wk, wv, freqs_cos, freqs_sin, out_0, out
                 op=ADD,
             )
 
-        def store(queue, g, j0, j1):
-            queue.dma_start(out=groups[g][1][:, j0:j1, :], in_=result[g][:, j0:j1, :])
+        def store(g, j0, j1):
+            nc.sync.dma_start(out=groups[g][1][:, j0:j1, :], in_=result[g][:, j0:j1, :])
 
         for j in range(TILES):
             load_x(j)
             load_w(j)
-        for u in range(PASSES, RAW_BUFS):
+        for u in range(PASSES, RAW_SLABS):
             load_w(u)
 
         table = keep.tile([P, 2, TILES, HD], F32)
-        pairs = TILES * HD // 2
+        angles = TILES * HD // 2
         nc.vector.tensor_copy(
             out=table[:, 0].rearrange("p j (i e) -> p (j i) e", e=2),
-            in_=cos_raw[:].unsqueeze(2).to_broadcast([P, pairs, 2]),
+            in_=cos_raw[:].unsqueeze(2).to_broadcast([P, angles, 2]),
         )
         nc.vector.tensor_tensor(
             out=table[:, 1].rearrange("p j (i e) -> p (j i) e", e=2),
-            in0=sin_raw[:].unsqueeze(2).to_broadcast([P, pairs, 2]),
-            in1=signs[:].unsqueeze(1).to_broadcast([P, pairs, 2]),
+            in0=sin_raw[:].unsqueeze(2).to_broadcast([P, angles, 2]),
+            in1=signs[:].unsqueeze(1).to_broadcast([P, angles, 2]),
             op=MULT,
         )
 
@@ -206,56 +206,55 @@ def tile_attention_pa_kernel(tc, x, wq, wk, wv, freqs_cos, freqs_sin, out_0, out
         for u in range(PASSES):
             if u + 1 < TILES:
                 transpose_x(u + 1)
+            pack_w(nc.scalar.copy, u, 0, FIRST_GROUP_SCALAR_COLS)
+            pack_w(nc.vector.tensor_copy, u, FIRST_GROUP_SCALAR_COLS, N)
+            if u > 0:
+                quantize_x(u - 1)
             pack_x(u)
-            pack_w(nc.scalar.copy, u, 0, HEAD_SCALAR_COLS)
-            pack_w(nc.vector.tensor_copy, u, HEAD_SCALAR_COLS, N)
-            quantize_x(u)
             quantize_w(u, 1)
-            for c in range(u):
-                multiply(c, u)
-            for j in range(u + 1):
-                multiply(u, j)
-        pack_w(nc.vector.tensor_copy, 4)
-        pack_w(nc.scalar.copy, 5)
-        pack_w(nc.vector.tensor_copy, 6)
-        quantize_and_multiply(4)
-        pack_w(nc.scalar.copy, 7)
-        pack_w(nc.vector.tensor_copy, 8)
+        pack_w(nc.vector.tensor_copy, PASSES)
+        quantize_x(TILES - 1)
+        for j in range(TILES):
+            for c in range(PASSES):
+                multiply(c, j)
 
-        pack_w(nc.scalar.copy, 9)
-        pack_w(nc.vector.tensor_copy, 10, N - 512, N)
-        for u in range(RAW_BUFS, slabs):
+        for u in range(PASSES + 1, LAST_VECTOR_SLAB, 2):
+            pack_w(nc.scalar.copy, u)
+            if u + 1 < LAST_VECTOR_SLAB:
+                pack_w(nc.vector.tensor_copy, u + 1)
+            if u < LEAD:
+                quantize_and_multiply(u - 1)
+        for u in range(RAW_SLABS, slabs):
             load_w(u)
 
-        last = len(groups) - 1
-        shared_from = N - SHARED_VECTOR_COLS
-        shared_cut = N - SHARED_VECTOR_COLS // 2 + 1
         for s in range(0, turns, 2):
             g, j = divmod(s, TILES)
-            u = s + 6
-            if 10 <= u < slabs:
-                if u > 10:
-                    pack_w(nc.scalar.copy, u)
-                pack_w(nc.scalar.copy, u + 1)
-            scale(s)
-            scale(s + 1)
+            u = s + LEAD
+            for slab in (u, u + 1):
+                if LAST_VECTOR_SLAB < slab < slabs:
+                    pack_w(nc.scalar.copy, slab)
+            rotation_products(s)
+            if s == 0:
+                pack_w(nc.vector.tensor_copy, LAST_VECTOR_SLAB)
+            rotation_products(s + 1)
             if u < slabs:
                 quantize_and_multiply(u)
-            if s < turns - 4:
-                combine(nc.gpsimd, s, 2)
+
+            if u + 2 < slabs:
+                rotation_sum(nc.gpsimd, s, 2)
                 if g >= 2:
-                    store(nc.sync, g, j, j + 2)
-                elif j == 2:
-                    store(nc.sync, g, 0, TILES)
-            elif s < turns - 2:
+                    store(g, j, j + 2)
+                elif j + 2 == TILES:
+                    store(g, 0, TILES)
+            elif u < slabs:
                 for b in range(2):
-                    combine(nc.gpsimd, s + 1 - b, 1)
+                    rotation_sum(nc.gpsimd, s + 1 - b, 1)
                     for jv in (2 * b, 2 * b + 1):
-                        nc.scalar.copy(out=out_tile(last)[:, jv, :], in_=acc[last, jv][:])
-                    store(nc.sync, last, 2 * b, 2 * b + 1)
-                    store(nc.sync, g, j + 1 - b, j + 2 - b)
-                    store(nc.sync, last, 2 * b + 1, 2 * b + 2)
+                        nc.scalar.copy(out=out_tile(v_group)[:, jv, :], in_=acc[v_group, jv][:])
+                    store(v_group, 2 * b, 2 * b + 1)
+                    store(g, j + 1 - b, j + 2 - b)
+                    store(v_group, 2 * b + 1, 2 * b + 2)
             else:
                 for b in range(2):
-                    combine(nc.vector, s + b, 1)
-                    store(nc.sync, g, j + b, j + b + 1)
+                    rotation_sum(nc.vector, s + b, 1)
+                    store(g, j + b, j + b + 1)

from contextlib import ExitStack

import concourse.mybir as mybir
from concourse.masks import make_identity

S, DIM, H, KV, HD = 512, 2048, 16, 4, 128
FLOPS = 2 * S * DIM * (H + 2 * KV) * HD

F32 = mybir.dt.float32
BF16 = mybir.dt.bfloat16
U32 = mybir.dt.uint32
U8 = mybir.dt.uint8
FP8X4 = mybir.dt.float8_e5m2_x4
MULT = mybir.AluOpType.mult
ADD = mybir.AluOpType.add

P = 128
PACK = 4
K_PASS = P * PACK
PASSES = DIM // K_PASS
TILES = S // P
N = 512
HEADS = N // HD
RUN = 4

RAW_SLABS = 16
PACKED_PAIRS = 5
CODE_PAIRS = 4
RESULT_TILES = 5
PRODUCT_PAIRS = 3

FIRST_GROUP_SCALAR_COLS = 192
LAST_VECTOR_SLAB = 10
LEAD = 6


def tile_attention_pa_kernel(tc, x, wq, wk, wv, freqs_cos, freqs_sin, out_0, out_1, out_2):
    nc = tc.nc

    x_rows = x[0].rearrange("(p j) k -> p j k", j=TILES)
    q_rows = out_0[0].rearrange("(p j) h d -> p j (h d)", j=TILES)
    k_rows = out_1[0].rearrange("(p j) h d -> p j (h d)", j=TILES)
    v_rows = out_2[0].rearrange("(p j) h d -> p j (h d)", j=TILES)
    groups = [(wk, k_rows)]
    groups += [(wq[:, n0 : n0 + N], q_rows[:, :, n0 : n0 + N]) for n0 in range(0, H * HD, N)]
    groups += [(wv, v_rows)]
    v_group = len(groups) - 1
    slabs = len(groups) * PASSES
    turns = v_group * TILES

    with ExitStack() as ctx:
        keep = ctx.enter_context(tc.tile_pool(name="keep", bufs=1))
        stream = ctx.enter_context(tc.tile_pool(name="stream", bufs=1))
        psum = ctx.enter_context(tc.psum_pool(name="psum", bufs=1))
        ctx.enter_context(tc.manual_schedule())

        ident = keep.tile([P, P], F32)
        make_identity(nc, ident[:])
        signs = keep.tile([P, 2], F32)
        nc.vector.memset(signs[:, 0:1], 1.0)
        nc.vector.memset(signs[:, 1:2], -1.0)

        cos_raw = keep.tile([P, TILES * HD // 2], BF16)
        sin_raw = keep.tile([P, TILES * HD // 2], BF16)
        nc.scalar.dma_start(out=cos_raw[:], in_=freqs_cos.rearrange("(p j) i -> p (j i)", j=TILES))
        nc.scalar.dma_start(out=sin_raw[:], in_=freqs_sin.rearrange("(p j) i -> p (j i)", j=TILES))

        w_raw, w_packed, w_codes, w_scales = {}, {}, {}, {}
        x_raw, x_turned, x_packed, acc, result, products = {}, {}, {}, {}, {}, {}
        x_codes = keep.tile([P, TILES, PASSES * P], U32, align_bytes=64)
        x_scales = keep.tile([P, TILES, PASSES * P], U8, align_bytes=64)

        def load_w(u):
            g, c = divmod(u, PASSES)
            w_raw[u] = stream.tile([P, PACK, N], BF16, name="w_raw", bufs=RAW_SLABS, align_bytes=64)
            rows = groups[g][0][c * K_PASS : (c + 1) * K_PASS, :]
            nc.sync.dma_start(out=w_raw[u][:], in_=rows.rearrange("(p t) n -> p t n", t=PACK))

        def load_x(j):
            x_raw[j] = stream.tile([P, DIM], BF16, name="x_raw", bufs=TILES, align_bytes=64)
            nc.sync.dma_start(out=x_raw[j][:], in_=x_rows[:, j, :])

        def pack_w(copy, u, c0=0, c1=N):
            pair, half = divmod(u, 2)
            if pair not in w_packed:
                w_packed[pair] = stream.tile([P, 2, N, PACK], BF16, name="w_packed", bufs=PACKED_PAIRS, align_bytes=64)
            copy(
                out=w_packed[pair][:, half][:, c0:c1, :].rearrange("p (c i) t -> p c t i", i=RUN),
                in_=w_raw[u][:, :, c0:c1].rearrange("p t (c i) -> p c t i", i=RUN),
            )

        def quantize_w(u, count):
            pair, half = divmod(u, 2)
            if pair not in w_codes:
                w_codes[pair] = stream.tile([P, 2 * N], U32, name="w_codes", bufs=CODE_PAIRS, align_bytes=64)
                w_scales[pair] = stream.tile([P, 2 * N], U8, name="w_scales", bufs=CODE_PAIRS, align_bytes=64)
            cols = slice(half * N, (half + count) * N)
            nc.vector.quantize_mx(
                out=w_codes[pair][:, cols].bitcast(FP8X4),
                scales=w_scales[pair][:, cols],
                in_=w_packed[pair][:, half : half + count].rearrange("p s n t -> p (s n t)"),
            )

        def bank(index):
            return psum.tile([P, N], F32, name="bank%d" % index)

        def transpose_x(j):
            words = x_raw[j][:].bitcast(F32)
            pass_words = K_PASS // 2
            x_turned[j] = []
            for half in range(2):
                turned = bank(TILES + 2 * (j % 2) + half)
                for slot in range(4):
                    w0 = (2 * half + slot // 2) * pass_words
                    nc.tensor.transpose(
                        turned[:, slot * P : (slot + 1) * P], words[:, w0 + slot % 2 : w0 + pass_words : 2], ident[:]
                    )
                x_turned[j].append(turned)

        def pack_x(j):
            x_packed[j] = stream.tile([P, DIM], BF16, name="x_packed", bufs=2, align_bytes=64)
            words = x_packed[j][:].bitcast(F32)
            for half, turned in enumerate(x_turned[j]):
                nc.scalar.copy(
                    out=words[:, half * N : (half + 1) * N].rearrange("p (c r o) -> p c r o", c=2, o=2),
                    in_=turned[:].rearrange("p (c o r) -> p c r o", c=2, o=2),
                )

        def quantize_x(j):
            nc.vector.quantize_mx(out=x_codes[:, j, :].bitcast(FP8X4), scales=x_scales[:, j, :], in_=x_packed[j][:])

        def multiply(u, j):
            g, c = divmod(u, PASSES)
            if c == 0:
                acc[g, j] = bank(TILES * (g % 2) + j)
            x_cols = slice(c * P, (c + 1) * P)
            w_cols = slice(u % 2 * N, (u % 2 + 1) * N)
            nc.tensor.matmul_mx(
                out=acc[g, j][:],
                lhsT=x_codes[:, j, x_cols].bitcast(FP8X4),
                lhsT_scale=x_scales[:, j, x_cols],
                rhs=w_codes[u // 2][:, w_cols].bitcast(FP8X4),
                rhs_scale=w_scales[u // 2][:, w_cols],
                start=(c == 0),
                stop=(c == PASSES - 1),
            )

        def quantize_and_multiply(u):
            quantize_w(u, 2)
            if u + 2 < slabs:
                order = [(slab, j) for slab in (u, u + 1) for j in range(TILES)]
            else:
                order = [(slab, j) for j in range(TILES) for slab in (u, u + 1)]
            for slab, j in order:
                multiply(slab, j)

        def out_tile(g):
            if g not in result:
                result[g] = stream.tile([P, TILES, N], F32, name="result", bufs=RESULT_TILES)
            return result[g]

        def rotation_products(s):
            g, j = divmod(s, TILES)
            if s % 2 == 0:
                products[s // 2] = stream.tile([P, 2, 2, N], F32, name="products", bufs=PRODUCT_PAIRS)
            nc.vector.tensor_tensor(
                out=products[s // 2][:, :, s % 2, :].rearrange("p w (h d) -> p w h d", h=HEADS),
                in0=acc[g, j][:].rearrange("p (h d) -> p h d", h=HEADS).unsqueeze(1).to_broadcast([P, 2, HEADS, HD]),
                in1=table[:, :, j, :].unsqueeze(2).to_broadcast([P, 2, HEADS, HD]),
                op=MULT,
            )

        def rotation_sum(engine, s, count):
            g, j = divmod(s, TILES)
            both = products[s // 2][:, :, s % 2 : s % 2 + count, :]
            engine.tensor_tensor(
                out=out_tile(g)[:, j : j + count, :].rearrange("p b (m e) -> p (b m) e", e=2),
                in0=both[:, 0].rearrange("p b (m e) -> p (b m) e", e=2),
                in1=both[:, 1].rearrange("p b (m e) -> p (b m) e", e=2)[:, :, ::-1],
                op=ADD,
            )

        def store(g, j0, j1):
            nc.sync.dma_start(out=groups[g][1][:, j0:j1, :], in_=result[g][:, j0:j1, :])

        for j in range(TILES):
            load_x(j)
            load_w(j)
        for u in range(PASSES, RAW_SLABS):
            load_w(u)

        table = keep.tile([P, 2, TILES, HD], F32)
        angles = TILES * HD // 2
        nc.vector.tensor_copy(
            out=table[:, 0].rearrange("p j (i e) -> p (j i) e", e=2),
            in_=cos_raw[:].unsqueeze(2).to_broadcast([P, angles, 2]),
        )
        nc.vector.tensor_tensor(
            out=table[:, 1].rearrange("p j (i e) -> p (j i) e", e=2),
            in0=sin_raw[:].unsqueeze(2).to_broadcast([P, angles, 2]),
            in1=signs[:].unsqueeze(1).to_broadcast([P, angles, 2]),
            op=MULT,
        )

        transpose_x(0)
        for u in range(PASSES):
            if u + 1 < TILES:
                transpose_x(u + 1)
            pack_w(nc.scalar.copy, u, 0, FIRST_GROUP_SCALAR_COLS)
            pack_w(nc.vector.tensor_copy, u, FIRST_GROUP_SCALAR_COLS, N)
            if u > 0:
                quantize_x(u - 1)
            pack_x(u)
            quantize_w(u, 1)
        pack_w(nc.vector.tensor_copy, PASSES)
        quantize_x(TILES - 1)
        for j in range(TILES):
            for c in range(PASSES):
                multiply(c, j)

        for u in range(PASSES + 1, LAST_VECTOR_SLAB, 2):
            pack_w(nc.scalar.copy, u)
            if u + 1 < LAST_VECTOR_SLAB:
                pack_w(nc.vector.tensor_copy, u + 1)
            if u < LEAD:
                quantize_and_multiply(u - 1)
        for u in range(RAW_SLABS, slabs):
            load_w(u)

        for s in range(0, turns, 2):
            g, j = divmod(s, TILES)
            u = s + LEAD
            for slab in (u, u + 1):
                if LAST_VECTOR_SLAB < slab < slabs:
                    pack_w(nc.scalar.copy, slab)
            rotation_products(s)
            if s == 0:
                pack_w(nc.vector.tensor_copy, LAST_VECTOR_SLAB)
            rotation_products(s + 1)
            if u < slabs:
                quantize_and_multiply(u)

            if u + 2 < slabs:
                rotation_sum(nc.gpsimd, s, 2)
                if g >= 2:
                    store(g, j, j + 2)
                elif j + 2 == TILES:
                    store(g, 0, TILES)
            elif u < slabs:
                for b in range(2):
                    rotation_sum(nc.gpsimd, s + 1 - b, 1)
                    for jv in (2 * b, 2 * b + 1):
                        nc.scalar.copy(out=out_tile(v_group)[:, jv, :], in_=acc[v_group, jv][:])
                    store(v_group, 2 * b, 2 * b + 1)
                    store(g, j + 1 - b, j + 2 - b)
                    store(v_group, 2 * b + 1, 2 * b + 2)
            else:
                for b in range(2):
                    rotation_sum(nc.vector, s + b, 1)
                    store(g, j + b, j + b + 1)
